import numpy as np
import ml_dtypes


def mxq(x, axis, fmt="e4m3"):
    dtype, down = {"e4m3": (ml_dtypes.float8_e4m3fn, 7), "e5m2": (ml_dtypes.float8_e5m2, 14)}[fmt]
    v = np.moveaxis(np.asarray(x, np.float32).astype(ml_dtypes.bfloat16).astype(np.float64), axis, -1)
    blocks = v.reshape(v.shape[:-1] + (-1, 32))
    amax = np.abs(blocks).max(-1, keepdims=True)
    byte = np.maximum(np.where(amax > 0, np.frexp(amax)[1] - 1 + 127, 0) - down, 1)
    scale = np.exp2(byte - 127.0)
    codes = (blocks / scale).astype(np.float32).astype(dtype).astype(np.float64)
    return np.moveaxis((codes * scale).reshape(v.shape), -1, axis)


WIDE = False


def mx_kscale(k):
    if not WIDE:
        return np.ones(k)
    levels = np.array([10, -10, 5, -5, 0])
    a = np.random.permutation(np.resize(levels, k // 512 * 4)).reshape(k // 512, 4)
    idx = np.arange(k)
    return np.exp2(a[idx // 512, idx % 128 // 32])


BF16 = ml_dtypes.bfloat16


def bf(x):
    return np.asarray(x, np.float32).astype(BF16)


def f64(x):
    return np.asarray(x).astype(np.float64)


B, T, D, DH, H, W = 1, 8192, 512, 64, 4, 512
ROPE_BASE = 10000.0
EPS = 1.1920929e-07


def rope(u):
    freqs = ROPE_BASE ** (-2.0 * np.arange(DH // 2) / DH)
    theta = np.arange(T)[:, None] * freqs[None, :]
    cos, sin = np.cos(theta), np.sin(theta)
    u1, u2 = u[..., 0::2], u[..., 1::2]
    return np.stack([u1 * cos - u2 * sin, u1 * sin + u2 * cos], axis=-1).reshape(u.shape)


def rmsnorm(u, w):
    return u * (1.0 / np.sqrt(np.mean(u * u, axis=-1, keepdims=True) + EPS)) * w


def setup_inputs():
    s = mx_kscale(D)
    return {"x": bf(np.random.standard_normal((B, T, D)) * s),
            "wq": bf(np.random.standard_normal((H * DH, D)) / np.sqrt(D) / s),
            "wkv": bf(np.random.standard_normal((2 * DH, D)) * 2.0 / np.sqrt(D) / s),
            "q_norm_w": bf(1.0 + 0.1 * np.random.standard_normal(DH)),
            "k_norm_w": bf(1.0 + 0.1 * np.random.standard_normal(DH))}


def reference(x, wq, wkv, q_norm_w, k_norm_w):
    xq = mxq(f64(x), 2, "e4m3")
    q = xq @ mxq(f64(wq), 1, "e4m3").T
    kv = xq @ mxq(f64(wkv), 1, "e4m3").T
    k, v = kv[..., :DH], kv[..., DH:]
    q = q.reshape(B, T, H, DH).transpose(0, 2, 1, 3)
    q_rot = rmsnorm(rope(q), f64(q_norm_w))
    k_rot = rmsnorm(rope(k), f64(k_norm_w))
    return q_rot, k_rot, v

@@ -1,0 +1,364 @@
+from contextlib import ExitStack
+
+import concourse.mybir as mybir
+from concourse.masks import make_identity
+
+FLOPS = 2 * 8192 * 512 * 384
+
+F32 = mybir.dt.float32
+BF16 = mybir.dt.bfloat16
+I32 = mybir.dt.int32
+U32 = mybir.dt.uint32
+U8 = mybir.dt.uint8
+FP8X4 = mybir.dt.float8_e4m3fn_x4
+ALU = mybir.AluOpType
+ACT = mybir.ActivationFunctionType
+
+P = 128
+D = 512
+DH = 64
+NPAIR = 32
+NT = 64
+CH = 8
+NCH = 8
+GR = 4
+NGR = 16
+LEAD = 2
+EPS = 1.1920929e-07
+TWO_PI = 6.283185307179586
+WCOLS = 704
+
+
+def turn_constants():
+    his = []
+    los = []
+    for i in range(NPAIR):
+        f = 10000.0 ** (-2.0 * i / DH) / TWO_PI
+        e = 0
+        while f * 2.0 ** e < 1.0:
+            e += 1
+        scale = 2.0 ** (e + 13)
+        hi = int(f * scale) / scale
+        his.append(hi)
+        los.append(f - hi)
+    return his, los
+
+
+def tile_attention_pa_t_kernel(tc, x, wq, wkv, q_norm_w, k_norm_w, out_0, out_1, out_2):
+    nc = tc.nc
+    with ExitStack() as ctx:
+        ctx.enter_context(tc.manual_schedule())
+        consts = ctx.enter_context(tc.tile_pool(name="consts", bufs=1))
+        xin = ctx.enter_context(tc.tile_pool(name="xin", bufs=3))
+        grps = ctx.enter_context(tc.tile_pool(name="grps", bufs=6))
+        small = ctx.enter_context(tc.tile_pool(name="small", bufs=4))
+        psum = ctx.enter_context(tc.psum_pool(name="psum", bufs=2))
+
+        xv = x[0].rearrange("(p j) k -> p j k", j=NT)
+        oqv = out_0[0].rearrange("h (p j) d -> p h j d", j=NT)
+        okv = out_1[0].rearrange("(p j) d -> p j d", j=NT)
+        ovv = out_2[0].rearrange("(p j) d -> p j d", j=NT)
+
+        ident = consts.tile([P, P], F32, name="ident")
+        perm = consts.tile([P, P], F32, name="perm")
+        ones = consts.tile([P, 1], F32, name="ones")
+        eps_t = consts.tile([P, 1], F32, name="eps_t")
+        gq_bf = consts.tile([P, DH], BF16, name="gq_bf")
+        gk_bf = consts.tile([P, DH], BF16, name="gk_bf")
+        gq = consts.tile([P, DH], F32, name="gq")
+        gk = consts.tile([P, DH], F32, name="gk")
+        wc = consts.tile([P, WCOLS], U32, name="wc", align_bytes=64)
+        ws = consts.tile([P, WCOLS], U8, name="ws", align_bytes=64)
+        xc = consts.tile([P, NT * P], U32, name="xc", align_bytes=64)
+        xs = consts.tile([P, NT * P], U8, name="xs", align_bytes=64)
+        base = consts.tile([P, NT, 2 * NPAIR], F32, name="base")
+        qtab = consts.tile([P, NT, 2 * DH], F32, name="qtab")
+        junk = consts.tile([P, DH], F32, name="junk")
+
+        x32 = {}
+        grp = {}
+
+        def ev_bank(e):
+            c, b = divmod(e, 4)
+            if b == 0:
+                grp[c] = grps.tile([P, 4096], BF16, name="grp", align_bytes=64)
+            xt = psum.tile([P, 4, P], F32, name="xt")
+            for a in range(2):
+                for u in range(2):
+                    nc.tensor.transpose(xt[:, 2 * a + u, :], x32[c][:, 2 * b + a, u * P:(u + 1) * P], ident[:])
+            grf = grp[c][:].bitcast(F32).rearrange("p (b a r u) -> p b a r u", b=4, a=2, u=2)
+            nc.scalar.copy(out=grf[:, b], in_=xt[:].rearrange("p (a u) r -> p a r u", u=2))
+
+        def qx(c):
+            cols = slice(c * CH * P, (c + 1) * CH * P)
+            nc.vector.quantize_mx(out=xc[:, cols].bitcast(FP8X4), scales=xs[:, cols], in_=grp[c][:])
+
+        def qgh(h):
+            js = slice(GR * h, GR * h + GR)
+            nc.vector.tensor_tensor(
+                out=qtab[:, js, :].rearrange("p j (c i e) -> p (j c) i e", c=2, e=2),
+                in0=base[:, js, :].rearrange("p j (c i) -> p (j c) i", c=2).unsqueeze(3).to_broadcast(
+                    [P, 2 * GR, NPAIR, 2]),
+                in1=gq[:].rearrange("p (i e) -> p i e", e=2).unsqueeze(1).to_broadcast([P, 2 * GR, NPAIR, 2]),
+                op=ALU.mult)
+
+        with tc.tile_pool(name="pro", bufs=1) as pro, tc.tile_pool(name="tabs", bufs=2) as tabs:
+            w_sb = pro.tile([P, 3, D], BF16, name="w_sb")
+            nc.scalar.dma_start(out=w_sb[:, 0:2, :], in_=wq.rearrange("(r p) k -> p r k", p=P))
+            nc.scalar.dma_start(out=w_sb[:, 2, :], in_=wkv)
+            nc.scalar.dma_start(out=gq_bf[:], in_=q_norm_w.partition_broadcast(P))
+            nc.scalar.dma_start(out=gk_bf[:], in_=k_norm_w.partition_broadcast(P))
+            for c in range(NCH):
+                x_sb = xin.tile([P, CH, D], BF16, name="x_sb")
+                nc.sync.dma_start(out=x_sb[:], in_=xv[:, c * CH:(c + 1) * CH, :])
+                x32[c] = x_sb[:].bitcast(F32)
+
+            make_identity(nc, ident[:])
+            t1i = pro.tile([P, NCH], I32, name="t1i")
+            nc.gpsimd.iota(t1i[:], pattern=[[CH, NCH]], base=0, channel_multiplier=NT)
+            j0i = pro.tile([P, CH], I32, name="j0i")
+            nc.gpsimd.iota(j0i[:], pattern=[[1, CH]], base=0, channel_multiplier=0)
+            nc.vector.memset(ones[:], 1.0)
+            nc.vector.memset(eps_t[:], EPS)
+            his, los = turn_constants()
+            fhi = pro.tile([P, NPAIR], F32, name="fhi")
+            flo = pro.tile([P, NPAIR], F32, name="flo")
+            for i in range(NPAIR):
+                nc.scalar.activation(out=fhi[:, i:i + 1], in_=ones[:], func=ACT.Copy, scale=his[i])
+            for i in range(NPAIR):
+                nc.scalar.activation(out=flo[:, i:i + 1], in_=ones[:], func=ACT.Copy, scale=los[i])
+            idv = ident[:].rearrange("p (i e) -> p e i", e=2)
+            pmv = perm[:].rearrange("p (i e) -> p e i", e=2)
+            nc.vector.tensor_copy(out=pmv[:, 0], in_=idv[:, 1])
+            nc.vector.tensor_copy(out=pmv[:, 1], in_=idv[:, 0])
+            t1f = pro.tile([P, NCH], F32, name="t1f")
+            j0f = pro.tile([P, CH], F32, name="j0f")
+            nc.vector.tensor_copy(out=t1f[:], in_=t1i[:])
+            nc.vector.tensor_copy(out=j0f[:], in_=j0i[:])
+
+            w32 = w_sb[:].bitcast(F32)
+            gw = pro.tile([P, WCOLS * 4], BF16, name="gw", align_bytes=64)
+            gwf = gw[:].bitcast(F32).rearrange("p (c u) -> p c u", u=2)
+            gwb = gw[:].rearrange("p (i e u f) -> p e i u f", e=2, u=2, f=2)
+
+            def w_transposes(dst, slot, r, mat):
+                for u in range(2):
+                    nc.tensor.transpose(dst[:, slot + u, :], w32[:, r, u * P:(u + 1) * P], mat[:])
+
+            def plain_cols(src, slot, cb):
+                nc.scalar.copy(out=gwf[:, cb:cb + P, :], in_=src[:, slot:slot + 2, :].rearrange("p u c -> p c u"))
+
+            def swapped_cols(src, slot, cb, n):
+                sv = src[:, slot:slot + 2, 0:n].rearrange("p u (i e) -> p e i u", e=2)
+                ov_ = gwf[:, cb:cb + n, :].rearrange("p (i e) u -> p e i u", e=2)
+                nc.vector.tensor_copy(out=ov_[:, 1], in_=sv[:, 1])
+                sb = src[:].bitcast(BF16)[:, slot:slot + 2, 0:2 * n].rearrange("p u (i e f) -> p e i u f", e=2, f=2)
+                nc.vector.tensor_scalar(out=gwb[:, 0, cb // 2:(cb + n) // 2], in0=sb[:, 0], scalar1=-1.0,
+                                        scalar2=None, op0=ALU.mult)
+
+            pa = psum.tile([P, 4, P], F32, name="xt")
+            w_transposes(pa, 0, 0, ident)
+            w_transposes(pa, 2, 1, ident)
+            pb = psum.tile([P, 4, P], F32, name="xt")
+            w_transposes(pb, 0, 2, ident)
+            w_transposes(pb, 2, 2, perm)
+            plain_cols(pa, 0, 256)
+            plain_cols(pa, 2, 384)
+            plain_cols(pb, 0, 576)
+            pc = psum.tile([P, 4, P], F32, name="xt")
+            w_transposes(pc, 0, 0, perm)
+            w_transposes(pc, 2, 1, perm)
+
+            def outer(dst, col, row):
+                nc.vector.tensor_tensor(out=dst[:], in0=col[:].unsqueeze(2).to_broadcast([P, 8, NPAIR]),
+                                        in1=row[:].unsqueeze(1).to_broadcast([P, 8, NPAIR]), op=ALU.mult)
+
+            def flat(t):
+                return t[:].rearrange("p a i -> p (a i)")
+
+            uh = pro.tile([P, 8, NPAIR], F32, name="uh")
+            ki = pro.tile([P, 8, NPAIR], I32, name="ki")
+            kf = pro.tile([P, 8, NPAIR], F32, name="kf")
+            na = pro.tile([P, 8, NPAIR], F32, name="na")
+            outer(uh, t1f, fhi)
+            nc.vector.tensor_copy(out=ki[:], in_=uh[:])
+            nc.vector.tensor_copy(out=kf[:], in_=ki[:])
+            nc.vector.tensor_tensor(out=uh[:], in0=uh[:], in1=kf[:], op=ALU.subtract)
+            outer(kf, t1f, flo)
+            nc.vector.tensor_tensor(out=uh[:], in0=uh[:], in1=kf[:], op=ALU.add)
+            nc.vector.scalar_tensor_tensor(out=flat(na), in0=flat(uh), scalar=0.5, in1=flat(uh), op0=ALU.is_ge,
+                                           op1=ALU.subtract)
+            bh = pro.tile([P, 8, NPAIR], F32, name="bh")
+            bl = pro.tile([P, 8, NPAIR], F32, name="bl")
+            bb = pro.tile([P, 8, 2, NPAIR], F32, name="bb")
+            nb = pro.tile([P, 16, NPAIR], F32, name="nb")
+            outer(bh, j0f, fhi)
+            outer(bl, j0f, flo)
+            nc.vector.tensor_tensor(out=bb[:, :, 0, :], in0=bh[:], in1=bl[:], op=ALU.add)
+            nc.vector.tensor_scalar(out=bb[:, :, 1, :], in0=bb[:, :, 0, :], scalar1=0.25, scalar2=None, op0=ALU.add)
+            bbf = bb[:].rearrange("p a c i -> p (a c i)")
+            nc.vector.scalar_tensor_tensor(out=flat(nb), in0=bbf, scalar=1.0, in1=bbf, op0=ALU.is_ge,
+                                           op1=ALU.subtract)
+
+            swapped_cols(pb, 2, 512, DH)
+            swapped_cols(pc, 0, 0, P)
+            swapped_cols(pc, 2, 128, P)
+            nc.vector.quantize_mx(out=wc[:, 0:512].bitcast(FP8X4), scales=ws[:, 0:512], in_=gw[:, 0:2048])
+            nc.vector.quantize_mx(out=wc[:, 512:640].bitcast(FP8X4), scales=ws[:, 512:640], in_=gw[:, 2048:2560])
+            nc.vector.quantize_mx(out=wc[:, 640:704].bitcast(FP8X4), scales=ws[:, 640:704], in_=gw[:, 2560:2816])
+            nc.vector.tensor_copy(out=gq[:], in_=gq_bf[:])
+            nc.vector.tensor_copy(out=gk[:], in_=gk_bf[:])
+
+            for e in range(12):
+                ev_bank(e)
+
+            for c in range(NCH):
+                nv = tabs.tile([P, 16, NPAIR], F32, name="nv")
+                nc.gpsimd.tensor_tensor(out=nv[:], in0=nb[:],
+                                        in1=na[:, c, :].unsqueeze(1).to_broadcast([P, 16, NPAIR]), op=ALU.add)
+                nc.vector.scalar_tensor_tensor(out=flat(nv), in0=flat(nv), scalar=-0.5, in1=flat(nv), op0=ALU.is_lt,
+                                               op1=ALU.add)
+                nc.scalar.activation(out=base[:, c * CH:(c + 1) * CH, :].rearrange("p j m -> p (j m)"), in_=flat(nv),
+                                     func=ACT.Sin, scale=-TWO_PI)
+                ev_bank(12 + c)
+                if c >= 1:
+                    qgh(c - 1)
+
+        for e in range(20, 24):
+            ev_bank(e)
+
+        work = ctx.enter_context(tc.tile_pool(name="work", bufs=2))
+        outs = ctx.enter_context(tc.tile_pool(name="outs", bufs=2))
+
+        ps_t = {}
+        ss_t = {}
+        rs_t = {}
+        ov_t = {}
+        oq_t = {}
+        ok_t = {}
+        tq_t = {}
+        tk_t = {}
+        pq_t = {}
+        pk_t = {}
+
+        def lhs_of(j):
+            return xc[:, j * P:(j + 1) * P].bitcast(FP8X4), xs[:, j * P:(j + 1) * P]
+
+        def m1(j):
+            ps = psum.tile([P, 384], F32, name="ps")
+            ps_t[j] = ps
+            lhs, lsc = lhs_of(j)
+            nc.tensor.matmul_mx(out=ps[:, 0:256], lhsT=lhs, lhsT_scale=lsc, rhs=wc[:, 256:512].bitcast(FP8X4),
+                                rhs_scale=ws[:, 256:512], start=True, stop=True)
+            nc.tensor.matmul_mx(out=ps[:, 256:384], lhsT=lhs, lhsT_scale=lsc, rhs=wc[:, 576:704].bitcast(FP8X4),
+                                rhs_scale=ws[:, 576:704], start=True, stop=True)
+
+        def squares(j):
+            q, i = divmod(j, GR)
+            c, jj = divmod(j, CH)
+            if i == 0:
+                ss_t[q] = small.tile([P, 5 * GR], F32, name="ss")
+            if jj == 0:
+                ov_t[c] = outs.tile([P, CH, DH], F32, name="ov", bufs=3)
+            ps = ps_t[j]
+            for h in range(5):
+                nc.scalar.activation(out=junk[:], in_=ps[:, h * DH:(h + 1) * DH], func=ACT.Square,
+                                     accum_out=ss_t[q][:, i * 5 + h:i * 5 + h + 1])
+            nc.scalar.copy(out=ov_t[c][:, jj, :], in_=ps[:, 320:384])
+
+        def root(q):
+            sd = small.tile([P, 5 * GR], F32, name="sd")
+            nc.scalar.activation(out=sd[:], in_=ss_t[q][:], func=ACT.Sqrt, scale=1.0 / DH, bias=eps_t[:])
+            ss_t[q] = sd
+
+        def recip(q):
+            rs_t[q] = small.tile([P, 5 * GR], F32, name="rs")
+            nc.vector.reciprocal(out=rs_t[q][:], in_=ss_t[q][:])
+
+        def m2(j, tag):
+            pq = psum.tile([P, 512], F32, name=tag)
+            pk = psum.tile([P, 2 * DH], F32, name="pk")
+            pq_t[j] = pq
+            pk_t[j] = pk
+            lhs, lsc = lhs_of(j)
+            nc.tensor.matmul_mx(out=pq[:], lhsT=lhs, lhsT_scale=lsc, rhs=wc[:, 0:512].bitcast(FP8X4),
+                                rhs_scale=ws[:, 0:512], start=True, stop=True)
+            nc.tensor.matmul_mx(out=pk[:], lhsT=lhs, lhsT_scale=lsc, rhs=wc[:, 512:640].bitcast(FP8X4),
+                                rhs_scale=ws[:, 512:640], start=True, stop=True)
+
+        def rope(j):
+            q, i = divmod(j, GR)
+            c, jj = divmod(j, CH)
+            if i == 0:
+                tq_t[q] = work.tile([P, GR, 512], F32, name="tq", bufs=3)
+            if jj == 0:
+                tk_t[c] = work.tile([P, CH, 2 * DH], F32, name="tk")
+            rs = rs_t[q]
+            pv = pq_t[j][:].rearrange("p (c h d) -> p h c d", c=2, h=4)
+            tv = tq_t[q][:, i, :].rearrange("p (c h d) -> p h c d", c=2, h=4)
+            for h in range(4):
+                nc.vector.scalar_tensor_tensor(out=tv[:, h], in0=pv[:, h], scalar=rs[:, i * 5 + h:i * 5 + h + 1],
+                                               in1=qtab[:, j, :].rearrange("p (c d) -> p c d", c=2), op0=ALU.mult,
+                                               op1=ALU.mult)
+            nc.vector.scalar_tensor_tensor(
+                out=tk_t[c][:, jj, :].rearrange("p (m e) -> p m e", e=2),
+                in0=pk_t[j][:].rearrange("p (m e) -> p m e", e=2), scalar=rs[:, i * 5 + 4:i * 5 + 5],
+                in1=base[:, j, :].unsqueeze(2).to_broadcast([P, 2 * NPAIR, 2]), op0=ALU.mult, op1=ALU.mult)
+
+        def add_q(q):
+            c, half = divmod(q, 2)
+            if half == 0:
+                oq_t[c] = outs.tile([P, 4, CH, DH], F32, name="oq")
+            tq = tq_t[q]
+            nc.gpsimd.tensor_tensor(
+                out=oq_t[c][:, :, half * GR:(half + 1) * GR, :].rearrange("p h j d -> p j h d"),
+                in0=tq[:, :, 0:256].rearrange("p j (h d) -> p j h d", h=4),
+                in1=tq[:, :, 256:512].rearrange("p j (h d) -> p j h d", h=4), op=ALU.add)
+
+        def add_k(c):
+            ok_t[c] = outs.tile([P, CH, DH], F32, name="ok")
+            uk = work.tile([P, CH, DH], F32, name="uk")
+            nc.gpsimd.tensor_tensor(out=uk[:], in0=tk_t[c][:, :, 0:DH], in1=tk_t[c][:, :, DH:2 * DH], op=ALU.add)
+            nc.gpsimd.tensor_tensor(out=ok_t[c][:], in0=uk[:], in1=gk[:].unsqueeze(1).to_broadcast([P, CH, DH]),
+                                    op=ALU.mult)
+
+        def store(c):
+            js = slice(c * CH, (c + 1) * CH)
+            nc.sync.dma_start(out=ovv[:, js, :], in_=ov_t[c][:])
+            nc.sync.dma_start(out=oqv[:, :, js, :], in_=oq_t[c][:])
+            nc.sync.dma_start(out=okv[:, js, :], in_=ok_t[c][:])
+
+        qx(0)
+        for j in range(LEAD * GR):
+            m1(j)
+            squares(j)
+            if j % GR == GR - 1:
+                root(j // GR)
+        for c in range(1, 6):
+            qx(c)
+        for h in range(7, 12):
+            qgh(h)
+
+        for q in range(NGR):
+            if q < 4:
+                ev_bank(24 + 2 * q)
+                ev_bank(25 + 2 * q)
+                qgh(12 + q)
+            if q == 4:
+                qx(6)
+                qx(7)
+            recip(q)
+            for i in range(GR):
+                j = q * GR + i
+                ja = j + LEAD * GR
+                m2(j, "pq" if (q < 4 or j % 2 == 0) else "xt")
+                if ja < NT:
+                    m1(ja)
+                    squares(ja)
+                rope(j)
+            if q + LEAD < NGR:
+                root(q + LEAD)
+            add_q(q)
+            if q % 2 == 1:
+                add_k(q // 2)
+                store(q // 2)

@@ -23,7 +23,9 @@ CH = 8
 NCH = 8
 GR = 4
 NGR = 16
-LEAD = 2
+SL = 4
+D1 = 2
+D2 = 3
 EPS = 1.1920929e-07
 TWO_PI = 6.283185307179586
 WCOLS = 704
@@ -52,7 +54,8 @@ def tile_attention_pa_t_kernel(tc, x, wq, wkv, q_norm_w, k_norm_w, out_0, out_1,
         xin = ctx.enter_context(tc.tile_pool(name="xin", bufs=3))
         grps = ctx.enter_context(tc.tile_pool(name="grps", bufs=6))
         small = ctx.enter_context(tc.tile_pool(name="small", bufs=4))
-        psum = ctx.enter_context(tc.psum_pool(name="psum", bufs=2))
+        junks = ctx.enter_context(tc.tile_pool(name="junks", bufs=8))
+        psum = ctx.enter_context(tc.psum_pool(name="psum", bufs=1))
 
         xv = x[0].rearrange("(p j) k -> p j k", j=NT)
         oqv = out_0[0].rearrange("h (p j) d -> p h j d", j=NT)
@@ -73,16 +76,18 @@ def tile_attention_pa_t_kernel(tc, x, wq, wkv, q_norm_w, k_norm_w, out_0, out_1,
         xs = consts.tile([P, NT * P], U8, name="xs", align_bytes=64)
         base = consts.tile([P, NT, 2 * NPAIR], F32, name="base")
         qtab = consts.tile([P, NT, 2 * DH], F32, name="qtab")
-        junk = consts.tile([P, DH], F32, name="junk")
 
         x32 = {}
         grp = {}
+
+        def bank(n, shape):
+            return psum.tile(shape, F32, name="b%d" % n)
 
         def ev_bank(e):
             c, b = divmod(e, 4)
             if b == 0:
                 grp[c] = grps.tile([P, 4096], BF16, name="grp", align_bytes=64)
-            xt = psum.tile([P, 4, P], F32, name="xt")
+            xt = bank(e % 4, [P, 4, P])
             for a in range(2):
                 for u in range(2):
                     nc.tensor.transpose(xt[:, 2 * a + u, :], x32[c][:, 2 * b + a, u * P:(u + 1) * P], ident[:])
@@ -102,7 +107,7 @@ def tile_attention_pa_t_kernel(tc, x, wq, wkv, q_norm_w, k_norm_w, out_0, out_1,
                 in1=gq[:].rearrange("p (i e) -> p i e", e=2).unsqueeze(1).to_broadcast([P, 2 * GR, NPAIR, 2]),
                 op=ALU.mult)
 
-        with tc.tile_pool(name="pro", bufs=1) as pro, tc.tile_pool(name="tabs", bufs=2) as tabs:
+        with tc.tile_pool(name="pro", bufs=1) as pro, tc.tile_pool(name="tabs", bufs=4) as tabs:
             w_sb = pro.tile([P, 3, D], BF16, name="w_sb")
             nc.scalar.dma_start(out=w_sb[:, 0:2, :], in_=wq.rearrange("(r p) k -> p r k", p=P))
             nc.scalar.dma_start(out=w_sb[:, 2, :], in_=wkv)
@@ -124,8 +129,7 @@ def tile_attention_pa_t_kernel(tc, x, wq, wkv, q_norm_w, k_norm_w, out_0, out_1,
             fhi = pro.tile([P, NPAIR], F32, name="fhi")
             flo = pro.tile([P, NPAIR], F32, name="flo")
             for i in range(NPAIR):
-                nc.scalar.activation(out=fhi[:, i:i + 1], in_=ones[:], func=ACT.Copy, scale=his[i])
-            for i in range(NPAIR):
+                nc.vector.memset(fhi[:, i:i + 1], his[i])
                 nc.scalar.activation(out=flo[:, i:i + 1], in_=ones[:], func=ACT.Copy, scale=los[i])
             idv = ident[:].rearrange("p (i e) -> p e i", e=2)
             pmv = perm[:].rearrange("p (i e) -> p e i", e=2)
@@ -150,24 +154,24 @@ def tile_attention_pa_t_kernel(tc, x, wq, wkv, q_norm_w, k_norm_w, out_0, out_1,
 
             def swapped_cols(src, slot, cb, n):
                 sv = src[:, slot:slot + 2, 0:n].rearrange("p u (i e) -> p e i u", e=2)
-                ov_ = gwf[:, cb:cb + n, :].rearrange("p (i e) u -> p e i u", e=2)
-                nc.vector.tensor_copy(out=ov_[:, 1], in_=sv[:, 1])
+                dv = gwf[:, cb:cb + n, :].rearrange("p (i e) u -> p e i u", e=2)
+                nc.vector.tensor_copy(out=dv[:, 1], in_=sv[:, 1])
                 sb = src[:].bitcast(BF16)[:, slot:slot + 2, 0:2 * n].rearrange("p u (i e f) -> p e i u f", e=2, f=2)
                 nc.vector.tensor_scalar(out=gwb[:, 0, cb // 2:(cb + n) // 2], in0=sb[:, 0], scalar1=-1.0,
                                         scalar2=None, op0=ALU.mult)
 
-            pa = psum.tile([P, 4, P], F32, name="xt")
+            pa = bank(4, [P, 4, P])
             w_transposes(pa, 0, 0, ident)
             w_transposes(pa, 2, 1, ident)
-            pb = psum.tile([P, 4, P], F32, name="xt")
+            pb = bank(5, [P, 4, P])
             w_transposes(pb, 0, 2, ident)
             w_transposes(pb, 2, 2, perm)
+            pc = bank(6, [P, 4, P])
+            w_transposes(pc, 0, 0, perm)
+            w_transposes(pc, 2, 1, perm)
             plain_cols(pa, 0, 256)
             plain_cols(pa, 2, 384)
             plain_cols(pb, 0, 576)
-            pc = psum.tile([P, 4, P], F32, name="xt")
-            w_transposes(pc, 0, 0, perm)
-            w_transposes(pc, 2, 1, perm)
 
             def outer(dst, col, row):
                 nc.vector.tensor_tensor(out=dst[:], in0=col[:].unsqueeze(2).to_broadcast([P, 8, NPAIR]),
@@ -179,53 +183,59 @@ def tile_attention_pa_t_kernel(tc, x, wq, wkv, q_norm_w, k_norm_w, out_0, out_1,
             uh = pro.tile([P, 8, NPAIR], F32, name="uh")
             ki = pro.tile([P, 8, NPAIR], I32, name="ki")
             kf = pro.tile([P, 8, NPAIR], F32, name="kf")
+            ul = pro.tile([P, 8, NPAIR], F32, name="ul")
             na = pro.tile([P, 8, NPAIR], F32, name="na")
-            outer(uh, t1f, fhi)
-            nc.vector.tensor_copy(out=ki[:], in_=uh[:])
-            nc.vector.tensor_copy(out=kf[:], in_=ki[:])
-            nc.vector.tensor_tensor(out=uh[:], in0=uh[:], in1=kf[:], op=ALU.subtract)
-            outer(kf, t1f, flo)
-            nc.vector.tensor_tensor(out=uh[:], in0=uh[:], in1=kf[:], op=ALU.add)
-            nc.vector.scalar_tensor_tensor(out=flat(na), in0=flat(uh), scalar=0.5, in1=flat(uh), op0=ALU.is_ge,
-                                           op1=ALU.subtract)
             bh = pro.tile([P, 8, NPAIR], F32, name="bh")
             bl = pro.tile([P, 8, NPAIR], F32, name="bl")
             bb = pro.tile([P, 8, 2, NPAIR], F32, name="bb")
             nb = pro.tile([P, 16, NPAIR], F32, name="nb")
-            outer(bh, j0f, fhi)
-            outer(bl, j0f, flo)
-            nc.vector.tensor_tensor(out=bb[:, :, 0, :], in0=bh[:], in1=bl[:], op=ALU.add)
-            nc.vector.tensor_scalar(out=bb[:, :, 1, :], in0=bb[:, :, 0, :], scalar1=0.25, scalar2=None, op0=ALU.add)
             bbf = bb[:].rearrange("p a c i -> p (a c i)")
+            outer(uh, t1f, fhi)
+            outer(bh, j0f, fhi)
+            nc.vector.tensor_copy(out=ki[:], in_=uh[:])
+            outer(bl, j0f, flo)
+            nc.vector.tensor_copy(out=kf[:], in_=ki[:])
+            outer(ul, t1f, flo)
+            nc.vector.tensor_tensor(out=uh[:], in0=uh[:], in1=kf[:], op=ALU.subtract)
+            nc.vector.tensor_tensor(out=bb[:, :, 0, :], in0=bh[:], in1=bl[:], op=ALU.add)
+            nc.vector.tensor_tensor(out=uh[:], in0=uh[:], in1=ul[:], op=ALU.add)
+            nc.vector.tensor_scalar(out=bb[:, :, 1, :], in0=bb[:, :, 0, :], scalar1=0.25, scalar2=None, op0=ALU.add)
+            nc.vector.scalar_tensor_tensor(out=flat(na), in0=flat(uh), scalar=0.5, in1=flat(uh), op0=ALU.is_ge,
+                                           op1=ALU.subtract)
             nc.vector.scalar_tensor_tensor(out=flat(nb), in0=bbf, scalar=1.0, in1=bbf, op0=ALU.is_ge,
                                            op1=ALU.subtract)
 
             swapped_cols(pb, 2, 512, DH)
             swapped_cols(pc, 0, 0, P)
             swapped_cols(pc, 2, 128, P)
-            nc.vector.quantize_mx(out=wc[:, 0:512].bitcast(FP8X4), scales=ws[:, 0:512], in_=gw[:, 0:2048])
-            nc.vector.quantize_mx(out=wc[:, 512:640].bitcast(FP8X4), scales=ws[:, 512:640], in_=gw[:, 2048:2560])
-            nc.vector.quantize_mx(out=wc[:, 640:704].bitcast(FP8X4), scales=ws[:, 640:704], in_=gw[:, 2560:2816])
-            nc.vector.tensor_copy(out=gq[:], in_=gq_bf[:])
-            nc.vector.tensor_copy(out=gk[:], in_=gk_bf[:])
 
-            for e in range(12):
+            for e in range(9):
                 ev_bank(e)
 
             for c in range(NCH):
                 nv = tabs.tile([P, 16, NPAIR], F32, name="nv")
                 nc.gpsimd.tensor_tensor(out=nv[:], in0=nb[:],
                                         in1=na[:, c, :].unsqueeze(1).to_broadcast([P, 16, NPAIR]), op=ALU.add)
+                if c >= 2:
+                    qgh(c - 2)
                 nc.vector.scalar_tensor_tensor(out=flat(nv), in0=flat(nv), scalar=-0.5, in1=flat(nv), op0=ALU.is_lt,
                                                op1=ALU.add)
+                if c == 0:
+                    nc.vector.quantize_mx(out=wc[:, 0:512].bitcast(FP8X4), scales=ws[:, 0:512], in_=gw[:, 0:2048])
+                    nc.vector.quantize_mx(out=wc[:, 512:640].bitcast(FP8X4), scales=ws[:, 512:640],
+                                          in_=gw[:, 2048:2560])
+                    nc.vector.quantize_mx(out=wc[:, 640:704].bitcast(FP8X4), scales=ws[:, 640:704],
+                                          in_=gw[:, 2560:2816])
+                    nc.vector.tensor_copy(out=gq[:], in_=gq_bf[:])
+                    nc.vector.tensor_copy(out=gk[:], in_=gk_bf[:])
                 nc.scalar.activation(out=base[:, c * CH:(c + 1) * CH, :].rearrange("p j m -> p (j m)"), in_=flat(nv),
                                      func=ACT.Sin, scale=-TWO_PI)
-                ev_bank(12 + c)
-                if c >= 1:
-                    qgh(c - 1)
+                ev_bank(9 + c)
 
-        for e in range(20, 24):
+        for e in range(17, 32):
             ev_bank(e)
+        for c in range(NCH):
+            qx(c)
 
         work = ctx.enter_context(tc.tile_pool(name="work", bufs=2))
         outs = ctx.enter_context(tc.tile_pool(name="outs", bufs=2))
@@ -245,7 +255,7 @@ def tile_attention_pa_t_kernel(tc, x, wq, wkv, q_norm_w, k_norm_w, out_0, out_1,
             return xc[:, j * P:(j + 1) * P].bitcast(FP8X4), xs[:, j * P:(j + 1) * P]
 
         def m1(j):
-            ps = psum.tile([P, 384], F32, name="ps")
+            ps = bank(4 + j % 3, [P, 384])
             ps_t[j] = ps
             lhs, lsc = lhs_of(j)
             nc.tensor.matmul_mx(out=ps[:, 0:256], lhsT=lhs, lhsT_scale=lsc, rhs=wc[:, 256:512].bitcast(FP8X4),
@@ -261,30 +271,30 @@ def tile_attention_pa_t_kernel(tc, x, wq, wkv, q_norm_w, k_norm_w, out_0, out_1,
             if jj == 0:
                 ov_t[c] = outs.tile([P, CH, DH], F32, name="ov", bufs=3)
             ps = ps_t[j]
+            junk = junks.tile([P, 5, DH], BF16, name="junk")
             for h in range(5):
-                nc.scalar.activation(out=junk[:], in_=ps[:, h * DH:(h + 1) * DH], func=ACT.Square,
+                nc.scalar.activation(out=junk[:, h, :], in_=ps[:, h * DH:(h + 1) * DH], func=ACT.Square,
                                      accum_out=ss_t[q][:, i * 5 + h:i * 5 + h + 1])
             nc.scalar.copy(out=ov_t[c][:, jj, :], in_=ps[:, 320:384])
+            if i == GR - 1:
+                rs_t[q] = small.tile([P, 5 * GR], F32, name="rs")
+                nc.scalar.activation(out=rs_t[q][:], in_=ss_t[q][:], func=ACT.Abs_reciprocal_sqrt, scale=1.0 / DH,
+                                     bias=eps_t[:])
 
-        def root(q):
-            sd = small.tile([P, 5 * GR], F32, name="sd")
-            nc.scalar.activation(out=sd[:], in_=ss_t[q][:], func=ACT.Sqrt, scale=1.0 / DH, bias=eps_t[:])
-            ss_t[q] = sd
-
-        def recip(q):
-            rs_t[q] = small.tile([P, 5 * GR], F32, name="rs")
-            nc.vector.reciprocal(out=rs_t[q][:], in_=ss_t[q][:])
-
-        def m2(j, tag):
-            pq = psum.tile([P, 512], F32, name=tag)
-            pk = psum.tile([P, 2 * DH], F32, name="pk")
+        def m2q(j):
+            pq = bank(j % 4, [P, 512])
             pq_t[j] = pq
-            pk_t[j] = pk
             lhs, lsc = lhs_of(j)
             nc.tensor.matmul_mx(out=pq[:], lhsT=lhs, lhsT_scale=lsc, rhs=wc[:, 0:512].bitcast(FP8X4),
                                 rhs_scale=ws[:, 0:512], start=True, stop=True)
-            nc.tensor.matmul_mx(out=pk[:], lhsT=lhs, lhsT_scale=lsc, rhs=wc[:, 512:640].bitcast(FP8X4),
-                                rhs_scale=ws[:, 512:640], start=True, stop=True)
+
+        def m2k(q):
+            pk = bank(7, [P, GR, 2 * DH])
+            pk_t[q] = pk
+            for i in range(GR):
+                lhs, lsc = lhs_of(q * GR + i)
+                nc.tensor.matmul_mx(out=pk[:, i, :], lhsT=lhs, lhsT_scale=lsc, rhs=wc[:, 512:640].bitcast(FP8X4),
+                                    rhs_scale=ws[:, 512:640], start=True, stop=True)
 
         def rope(j):
             q, i = divmod(j, GR)
@@ -302,63 +312,72 @@ def tile_attention_pa_t_kernel(tc, x, wq, wkv, q_norm_w, k_norm_w, out_0, out_1,
                                                op1=ALU.mult)
             nc.vector.scalar_tensor_tensor(
                 out=tk_t[c][:, jj, :].rearrange("p (m e) -> p m e", e=2),
-                in0=pk_t[j][:].rearrange("p (m e) -> p m e", e=2), scalar=rs[:, i * 5 + 4:i * 5 + 5],
+                in0=pk_t[q][:, i, :].rearrange("p (m e) -> p m e", e=2), scalar=rs[:, i * 5 + 4:i * 5 + 5],
                 in1=base[:, j, :].unsqueeze(2).to_broadcast([P, 2 * NPAIR, 2]), op0=ALU.mult, op1=ALU.mult)
 
-        def add_q(q):
+        def add_q(eng, q, lo, hi):
             c, half = divmod(q, 2)
-            if half == 0:
+            if half == 0 and lo == 0:
                 oq_t[c] = outs.tile([P, 4, CH, DH], F32, name="oq")
             tq = tq_t[q]
-            nc.gpsimd.tensor_tensor(
-                out=oq_t[c][:, :, half * GR:(half + 1) * GR, :].rearrange("p h j d -> p j h d"),
-                in0=tq[:, :, 0:256].rearrange("p j (h d) -> p j h d", h=4),
-                in1=tq[:, :, 256:512].rearrange("p j (h d) -> p j h d", h=4), op=ALU.add)
+            eng.tensor_tensor(
+                out=oq_t[c][:, :, half * GR + lo:half * GR + hi, :].rearrange("p h j d -> p j h d"),
+                in0=tq[:, lo:hi, 0:256].rearrange("p j (h d) -> p j h d", h=4),
+                in1=tq[:, lo:hi, 256:512].rearrange("p j (h d) -> p j h d", h=4), op=ALU.add)
 
-        def add_k(c):
-            ok_t[c] = outs.tile([P, CH, DH], F32, name="ok")
+        def add_k(c, lo, hi):
+            if lo == 0:
+                ok_t[c] = outs.tile([P, CH, DH], F32, name="ok")
             uk = work.tile([P, CH, DH], F32, name="uk")
-            nc.gpsimd.tensor_tensor(out=uk[:], in0=tk_t[c][:, :, 0:DH], in1=tk_t[c][:, :, DH:2 * DH], op=ALU.add)
-            nc.gpsimd.tensor_tensor(out=ok_t[c][:], in0=uk[:], in1=gk[:].unsqueeze(1).to_broadcast([P, CH, DH]),
-                                    op=ALU.mult)
+            nc.gpsimd.tensor_tensor(out=uk[:, lo:hi, :], in0=tk_t[c][:, lo:hi, 0:DH], in1=tk_t[c][:, lo:hi, DH:2 * DH],
+                                    op=ALU.add)
+            nc.gpsimd.tensor_tensor(out=ok_t[c][:, lo:hi, :], in0=uk[:, lo:hi, :],
+                                    in1=gk[:].unsqueeze(1).to_broadcast([P, hi - lo, DH]), op=ALU.mult)
 
-        def store(c):
-            js = slice(c * CH, (c + 1) * CH)
-            nc.sync.dma_start(out=ovv[:, js, :], in_=ov_t[c][:])
-            nc.sync.dma_start(out=oqv[:, :, js, :], in_=oq_t[c][:])
-            nc.sync.dma_start(out=okv[:, js, :], in_=ok_t[c][:])
+        def store(c, lo, hi):
+            js = slice(c * CH + lo, c * CH + hi)
+            nc.sync.dma_start(out=oqv[:, :, js, :], in_=oq_t[c][:, :, lo:hi, :])
+            nc.sync.dma_start(out=okv[:, js, :], in_=ok_t[c][:, lo:hi, :])
 
-        qx(0)
-        for j in range(LEAD * GR):
-            m1(j)
-            squares(j)
-            if j % GR == GR - 1:
-                root(j // GR)
-        for c in range(1, 6):
-            qx(c)
-        for h in range(7, 12):
-            qgh(h)
+        for a in range(D1):
+            m1(a)
+        for a in range(SL):
+            m1(a + D1)
+            squares(a)
+        for j in range(D2):
+            m2q(j)
+        m2k(0)
 
         for q in range(NGR):
-            if q < 4:
-                ev_bank(24 + 2 * q)
-                ev_bank(25 + 2 * q)
-                qgh(12 + q)
-            if q == 4:
-                qx(6)
-                qx(7)
-            recip(q)
+            if 6 + q < NGR:
+                qgh(6 + q)
             for i in range(GR):
                 j = q * GR + i
-                ja = j + LEAD * GR
-                m2(j, "pq" if (q < 4 or j % 2 == 0) else "xt")
-                if ja < NT:
-                    m1(ja)
-                    squares(ja)
+                a = j + SL
+                if i == 0 and q > 0:
+                    m2k(q)
+                if a + D1 < NT:
+                    m1(a + D1)
+                if j + D2 < NT:
+                    m2q(j + D2)
+                if a < NT:
+                    squares(a)
+                    if a % CH == CH - 1:
+                        nc.sync.dma_start(out=ovv[:, a - CH + 1:a + 1, :], in_=ov_t[a // CH][:])
                 rope(j)
-            if q + LEAD < NGR:
-                root(q + LEAD)
-            add_q(q)
-            if q % 2 == 1:
-                add_k(q // 2)
-                store(q // 2)
+                if q == NGR - 1 and i == 1:
+                    add_q(nc.gpsimd, q, 0, 2)
+            c = q // 2
+            if q < NGR - 2:
+                add_q(nc.gpsimd, q, 0, GR)
+                if q % 2 == 1:
+                    add_k(c, 0, CH)
+                    store(c, 0, CH)
+            elif q == NGR - 2:
+                add_q(nc.gpsimd, q, 0, GR)
+                add_k(c, 0, GR)
+                store(c, 0, GR)
+            else:
+                add_q(nc.vector, q, 2, GR)
+                add_k(c, GR, CH)
+                store(c, GR, CH)

@@ -310,10 +310,16 @@ def tile_attention_pa_t_kernel(tc, x, wq, wkv, q_norm_w, k_norm_w, out_0, out_1,
                 nc.vector.scalar_tensor_tensor(out=tv[:, h], in0=pv[:, h], scalar=rs[:, i * 5 + h:i * 5 + h + 1],
                                                in1=qtab[:, j, :].rearrange("p (c d) -> p c d", c=2), op0=ALU.mult,
                                                op1=ALU.mult)
-            nc.vector.scalar_tensor_tensor(
-                out=tk_t[c][:, jj, :].rearrange("p (m e) -> p m e", e=2),
-                in0=pk_t[q][:, i, :].rearrange("p (m e) -> p m e", e=2), scalar=rs[:, i * 5 + 4:i * 5 + 5],
-                in1=base[:, j, :].unsqueeze(2).to_broadcast([P, 2 * NPAIR, 2]), op0=ALU.mult, op1=ALU.mult)
+
+        def rope_k(q):
+            rs = rs_t[q]
+            for i in range(GR):
+                j = q * GR + i
+                c, jj = divmod(j, CH)
+                nc.vector.scalar_tensor_tensor(
+                    out=tk_t[c][:, jj, :].rearrange("p (m e) -> p m e", e=2),
+                    in0=pk_t[q][:, i, :].rearrange("p (m e) -> p m e", e=2), scalar=rs[:, i * 5 + 4:i * 5 + 5],
+                    in1=base[:, j, :].unsqueeze(2).to_broadcast([P, 2 * NPAIR, 2]), op0=ALU.mult, op1=ALU.mult)
 
         def add_q(eng, q, lo, hi):
             c, half = divmod(q, 2)
@@ -341,12 +347,12 @@ def tile_attention_pa_t_kernel(tc, x, wq, wkv, q_norm_w, k_norm_w, out_0, out_1,
 
         for a in range(D1):
             m1(a)
-        for a in range(SL):
-            m1(a + D1)
-            squares(a)
         for j in range(D2):
             m2q(j)
         m2k(0)
+        for a in range(SL):
+            m1(a + D1)
+            squares(a)
 
         for q in range(NGR):
             if 6 + q < NGR:
@@ -367,6 +373,7 @@ def tile_attention_pa_t_kernel(tc, x, wq, wkv, q_norm_w, k_norm_w, out_0, out_1,
                 rope(j)
                 if q == NGR - 1 and i == 1:
                     add_q(nc.gpsimd, q, 0, 2)
+            rope_k(q)
             c = q // 2
             if q < NGR - 2:
                 add_q(nc.gpsimd, q, 0, GR)

@@ -23,7 +23,7 @@ CH = 8
 NCH = 8
 GR = 4
 NGR = 16
-SL = 4
+SL = 14
 D1 = 2
 D2 = 3
 EPS = 1.1920929e-07
@@ -52,8 +52,8 @@ def tile_attention_pa_t_kernel(tc, x, wq, wkv, q_norm_w, k_norm_w, out_0, out_1,
         ctx.enter_context(tc.manual_schedule())
         consts = ctx.enter_context(tc.tile_pool(name="consts", bufs=1))
         xin = ctx.enter_context(tc.tile_pool(name="xin", bufs=3))
-        grps = ctx.enter_context(tc.tile_pool(name="grps", bufs=6))
-        small = ctx.enter_context(tc.tile_pool(name="small", bufs=4))
+        grps = ctx.enter_context(tc.tile_pool(name="grps", bufs=5))
+        small = ctx.enter_context(tc.tile_pool(name="small", bufs=8))
         junks = ctx.enter_context(tc.tile_pool(name="junks", bufs=8))
         psum = ctx.enter_context(tc.psum_pool(name="psum", bufs=1))
 
@@ -83,7 +83,7 @@ def tile_attention_pa_t_kernel(tc, x, wq, wkv, q_norm_w, k_norm_w, out_0, out_1,
         def bank(n, shape):
             return psum.tile(shape, F32, name="b%d" % n)
 
-        def ev_bank(e):
+        def ev_bank(e, on_vector=False):
             c, b = divmod(e, 4)
             if b == 0:
                 grp[c] = grps.tile([P, 4096], BF16, name="grp", align_bytes=64)
@@ -92,7 +92,10 @@ def tile_attention_pa_t_kernel(tc, x, wq, wkv, q_norm_w, k_norm_w, out_0, out_1,
                 for u in range(2):
                     nc.tensor.transpose(xt[:, 2 * a + u, :], x32[c][:, 2 * b + a, u * P:(u + 1) * P], ident[:])
             grf = grp[c][:].bitcast(F32).rearrange("p (b a r u) -> p b a r u", b=4, a=2, u=2)
-            nc.scalar.copy(out=grf[:, b], in_=xt[:].rearrange("p (a u) r -> p a r u", u=2))
+            if on_vector:
+                nc.vector.tensor_copy(out=grf[:, b], in_=xt[:].rearrange("p (a u) r -> p a r u", u=2))
+            else:
+                nc.scalar.copy(out=grf[:, b], in_=xt[:].rearrange("p (a u) r -> p a r u", u=2))
 
         def qx(c):
             cols = slice(c * CH * P, (c + 1) * CH * P)
@@ -232,9 +235,9 @@ def tile_attention_pa_t_kernel(tc, x, wq, wkv, q_norm_w, k_norm_w, out_0, out_1,
                                      func=ACT.Sin, scale=-TWO_PI)
                 ev_bank(9 + c)
 
-        for e in range(17, 32):
+        for e in range(17, 20):
             ev_bank(e)
-        for c in range(NCH):
+        for c in range(5):
             qx(c)
 
         work = ctx.enter_context(tc.tile_pool(name="work", bufs=2))
@@ -269,7 +272,7 @@ def tile_attention_pa_t_kernel(tc, x, wq, wkv, q_norm_w, k_norm_w, out_0, out_1,
             if i == 0:
                 ss_t[q] = small.tile([P, 5 * GR], F32, name="ss")
             if jj == 0:
-                ov_t[c] = outs.tile([P, CH, DH], F32, name="ov", bufs=3)
+                ov_t[c] = outs.tile([P, CH, DH], F32, name="ov", bufs=4)
             ps = ps_t[j]
             junk = junks.tile([P, 5, DH], BF16, name="junk")
             for h in range(5):
@@ -310,16 +313,10 @@ def tile_attention_pa_t_kernel(tc, x, wq, wkv, q_norm_w, k_norm_w, out_0, out_1,
                 nc.vector.scalar_tensor_tensor(out=tv[:, h], in0=pv[:, h], scalar=rs[:, i * 5 + h:i * 5 + h + 1],
                                                in1=qtab[:, j, :].rearrange("p (c d) -> p c d", c=2), op0=ALU.mult,
                                                op1=ALU.mult)
-
-        def rope_k(q):
-            rs = rs_t[q]
-            for i in range(GR):
-                j = q * GR + i
-                c, jj = divmod(j, CH)
-                nc.vector.scalar_tensor_tensor(
-                    out=tk_t[c][:, jj, :].rearrange("p (m e) -> p m e", e=2),
-                    in0=pk_t[q][:, i, :].rearrange("p (m e) -> p m e", e=2), scalar=rs[:, i * 5 + 4:i * 5 + 5],
-                    in1=base[:, j, :].unsqueeze(2).to_broadcast([P, 2 * NPAIR, 2]), op0=ALU.mult, op1=ALU.mult)
+            nc.vector.scalar_tensor_tensor(
+                out=tk_t[c][:, jj, :].rearrange("p (m e) -> p m e", e=2),
+                in0=pk_t[q][:, i, :].rearrange("p (m e) -> p m e", e=2), scalar=rs[:, i * 5 + 4:i * 5 + 5],
+                in1=base[:, j, :].unsqueeze(2).to_broadcast([P, 2 * NPAIR, 2]), op0=ALU.mult, op1=ALU.mult)
 
         def add_q(eng, q, lo, hi):
             c, half = divmod(q, 2)
@@ -345,35 +342,43 @@ def tile_attention_pa_t_kernel(tc, x, wq, wkv, q_norm_w, k_norm_w, out_0, out_1,
             nc.sync.dma_start(out=oqv[:, :, js, :], in_=oq_t[c][:, :, lo:hi, :])
             nc.sync.dma_start(out=okv[:, js, :], in_=ok_t[c][:, lo:hi, :])
 
+        def scalar_tile(a):
+            if a + D1 < NT:
+                m1(a + D1)
+            squares(a)
+            if a % CH == CH - 1:
+                nc.sync.dma_start(out=ovv[:, a - CH + 1:a + 1, :], in_=ov_t[a // CH][:])
+
         for a in range(D1):
             m1(a)
+        for k in range(12):
+            ev_bank(20 + k, on_vector=True)
+            if k in (5, 9):
+                qx(4 + k // 4)
+            scalar_tile(k)
+        qgh(6)
+        qx(7)
+        for a in range(12, SL):
+            scalar_tile(a)
         for j in range(D2):
             m2q(j)
         m2k(0)
-        for a in range(SL):
-            m1(a + D1)
-            squares(a)
 
         for q in range(NGR):
-            if 6 + q < NGR:
-                qgh(6 + q)
+            if 7 + q < NGR:
+                qgh(7 + q)
             for i in range(GR):
                 j = q * GR + i
                 a = j + SL
+                if a < NT:
+                    scalar_tile(a)
                 if i == 0 and q > 0:
                     m2k(q)
-                if a + D1 < NT:
-                    m1(a + D1)
                 if j + D2 < NT:
                     m2q(j + D2)
-                if a < NT:
-                    squares(a)
-                    if a % CH == CH - 1:
-                        nc.sync.dma_start(out=ovv[:, a - CH + 1:a + 1, :], in_=ov_t[a // CH][:])
                 rope(j)
                 if q == NGR - 1 and i == 1:
                     add_q(nc.gpsimd, q, 0, 2)
-            rope_k(q)
             c = q // 2
             if q < NGR - 2:
                 add_q(nc.gpsimd, q, 0, GR)

@@ -23,7 +23,7 @@ CH = 8
 NCH = 8
 GR = 4
 NGR = 16
-SL = 14
+SL = 4
 D1 = 2
 D2 = 3
 EPS = 1.1920929e-07
@@ -52,8 +52,8 @@ def tile_attention_pa_t_kernel(tc, x, wq, wkv, q_norm_w, k_norm_w, out_0, out_1,
         ctx.enter_context(tc.manual_schedule())
         consts = ctx.enter_context(tc.tile_pool(name="consts", bufs=1))
         xin = ctx.enter_context(tc.tile_pool(name="xin", bufs=3))
-        grps = ctx.enter_context(tc.tile_pool(name="grps", bufs=5))
-        small = ctx.enter_context(tc.tile_pool(name="small", bufs=8))
+        grps = ctx.enter_context(tc.tile_pool(name="grps", bufs=6))
+        small = ctx.enter_context(tc.tile_pool(name="small", bufs=4))
         junks = ctx.enter_context(tc.tile_pool(name="junks", bufs=8))
         psum = ctx.enter_context(tc.psum_pool(name="psum", bufs=1))
 
@@ -83,7 +83,7 @@ def tile_attention_pa_t_kernel(tc, x, wq, wkv, q_norm_w, k_norm_w, out_0, out_1,
         def bank(n, shape):
             return psum.tile(shape, F32, name="b%d" % n)
 
-        def ev_bank(e, on_vector=False):
+        def ev_bank(e):
             c, b = divmod(e, 4)
             if b == 0:
                 grp[c] = grps.tile([P, 4096], BF16, name="grp", align_bytes=64)
@@ -92,10 +92,7 @@ def tile_attention_pa_t_kernel(tc, x, wq, wkv, q_norm_w, k_norm_w, out_0, out_1,
                 for u in range(2):
                     nc.tensor.transpose(xt[:, 2 * a + u, :], x32[c][:, 2 * b + a, u * P:(u + 1) * P], ident[:])
             grf = grp[c][:].bitcast(F32).rearrange("p (b a r u) -> p b a r u", b=4, a=2, u=2)
-            if on_vector:
-                nc.vector.tensor_copy(out=grf[:, b], in_=xt[:].rearrange("p (a u) r -> p a r u", u=2))
-            else:
-                nc.scalar.copy(out=grf[:, b], in_=xt[:].rearrange("p (a u) r -> p a r u", u=2))
+            nc.scalar.copy(out=grf[:, b], in_=xt[:].rearrange("p (a u) r -> p a r u", u=2))
 
         def qx(c):
             cols = slice(c * CH * P, (c + 1) * CH * P)
@@ -235,9 +232,9 @@ def tile_attention_pa_t_kernel(tc, x, wq, wkv, q_norm_w, k_norm_w, out_0, out_1,
                                      func=ACT.Sin, scale=-TWO_PI)
                 ev_bank(9 + c)
 
-        for e in range(17, 20):
+        for e in range(17, 32):
             ev_bank(e)
-        for c in range(5):
+        for c in range(NCH):
             qx(c)
 
         work = ctx.enter_context(tc.tile_pool(name="work", bufs=2))
@@ -272,7 +269,7 @@ def tile_attention_pa_t_kernel(tc, x, wq, wkv, q_norm_w, k_norm_w, out_0, out_1,
             if i == 0:
                 ss_t[q] = small.tile([P, 5 * GR], F32, name="ss")
             if jj == 0:
-                ov_t[c] = outs.tile([P, CH, DH], F32, name="ov", bufs=4)
+                ov_t[c] = outs.tile([P, CH, DH], F32, name="ov", bufs=3)
             ps = ps_t[j]
             junk = junks.tile([P, 5, DH], BF16, name="junk")
             for h in range(5):
@@ -342,54 +339,41 @@ def tile_attention_pa_t_kernel(tc, x, wq, wkv, q_norm_w, k_norm_w, out_0, out_1,
             nc.sync.dma_start(out=oqv[:, :, js, :], in_=oq_t[c][:, :, lo:hi, :])
             nc.sync.dma_start(out=okv[:, js, :], in_=ok_t[c][:, lo:hi, :])
 
-        def scalar_tile(a):
-            if a + D1 < NT:
-                m1(a + D1)
-            squares(a)
-            if a % CH == CH - 1:
-                nc.sync.dma_start(out=ovv[:, a - CH + 1:a + 1, :], in_=ov_t[a // CH][:])
-
         for a in range(D1):
             m1(a)
-        for k in range(12):
-            ev_bank(20 + k, on_vector=True)
-            if k in (5, 9):
-                qx(4 + k // 4)
-            scalar_tile(k)
-        qgh(6)
-        qx(7)
-        for a in range(12, SL):
-            scalar_tile(a)
+        for a in range(SL):
+            m1(a + D1)
+            squares(a)
         for j in range(D2):
             m2q(j)
         m2k(0)
 
         for q in range(NGR):
-            if 7 + q < NGR:
-                qgh(7 + q)
+            if 6 + q < NGR:
+                qgh(6 + q)
             for i in range(GR):
                 j = q * GR + i
                 a = j + SL
-                if a < NT:
-                    scalar_tile(a)
+                if a + D1 < NT:
+                    m1(a + D1)
                 if i == 0 and q > 0:
                     m2k(q)
                 if j + D2 < NT:
                     m2q(j + D2)
+                if a < NT:
+                    squares(a)
+                    if a % CH == CH - 1:
+                        nc.sync.dma_start(out=ovv[:, a - CH + 1:a + 1, :], in_=ov_t[a // CH][:])
                 rope(j)
-                if q == NGR - 1 and i == 1:
-                    add_q(nc.gpsimd, q, 0, 2)
             c = q // 2
+            add_q(nc.vector if (q % 4 == 3 or q >= NGR - 2) else nc.gpsimd, q, 0, GR)
             if q < NGR - 2:
-                add_q(nc.gpsimd, q, 0, GR)
                 if q % 2 == 1:
                     add_k(c, 0, CH)
                     store(c, 0, CH)
             elif q == NGR - 2:
-                add_q(nc.gpsimd, q, 0, GR)
                 add_k(c, 0, GR)
                 store(c, 0, GR)
             else:
-                add_q(nc.vector, q, 2, GR)
                 add_k(c, GR, CH)
                 store(c, GR, CH)

from contextlib import ExitStack

import concourse.mybir as mybir
from concourse.masks import make_identity

FLOPS = 2 * 8192 * 512 * 384

F32 = mybir.dt.float32
BF16 = mybir.dt.bfloat16
I32 = mybir.dt.int32
U32 = mybir.dt.uint32
U8 = mybir.dt.uint8
FP8X4 = mybir.dt.float8_e4m3fn_x4
ALU = mybir.AluOpType
ACT = mybir.ActivationFunctionType

P = 128
D = 512
DH = 64
NPAIR = 32
NT = 64
CH = 8
NCH = 8
GR = 4
NGR = 16
SL = 4
D1 = 2
D2 = 3
EPS = 1.1920929e-07
TWO_PI = 6.283185307179586
WCOLS = 704


def turn_constants():
    his = []
    los = []
    for i in range(NPAIR):
        f = 10000.0 ** (-2.0 * i / DH) / TWO_PI
        e = 0
        while f * 2.0 ** e < 1.0:
            e += 1
        scale = 2.0 ** (e + 13)
        hi = int(f * scale) / scale
        his.append(hi)
        los.append(f - hi)
    return his, los


def tile_attention_pa_t_kernel(tc, x, wq, wkv, q_norm_w, k_norm_w, out_0, out_1, out_2):
    nc = tc.nc
    with ExitStack() as ctx:
        ctx.enter_context(tc.manual_schedule())
        consts = ctx.enter_context(tc.tile_pool(name="consts", bufs=1))
        xin = ctx.enter_context(tc.tile_pool(name="xin", bufs=3))
        grps = ctx.enter_context(tc.tile_pool(name="grps", bufs=6))
        small = ctx.enter_context(tc.tile_pool(name="small", bufs=4))
        junks = ctx.enter_context(tc.tile_pool(name="junks", bufs=8))
        psum = ctx.enter_context(tc.psum_pool(name="psum", bufs=1))

        xv = x[0].rearrange("(p j) k -> p j k", j=NT)
        oqv = out_0[0].rearrange("h (p j) d -> p h j d", j=NT)
        okv = out_1[0].rearrange("(p j) d -> p j d", j=NT)
        ovv = out_2[0].rearrange("(p j) d -> p j d", j=NT)

        ident = consts.tile([P, P], F32, name="ident")
        perm = consts.tile([P, P], F32, name="perm")
        ones = consts.tile([P, 1], F32, name="ones")
        eps_t = consts.tile([P, 1], F32, name="eps_t")
        gq_bf = consts.tile([P, DH], BF16, name="gq_bf")
        gk_bf = consts.tile([P, DH], BF16, name="gk_bf")
        gq = consts.tile([P, DH], F32, name="gq")
        gk = consts.tile([P, DH], F32, name="gk")
        wc = consts.tile([P, WCOLS], U32, name="wc", align_bytes=64)
        ws = consts.tile([P, WCOLS], U8, name="ws", align_bytes=64)
        xc = consts.tile([P, NT * P], U32, name="xc", align_bytes=64)
        xs = consts.tile([P, NT * P], U8, name="xs", align_bytes=64)
        base = consts.tile([P, NT, 2 * NPAIR], F32, name="base")
        qtab = consts.tile([P, NT, 2 * DH], F32, name="qtab")

        x32 = {}
        grp = {}

        def bank(n, shape):
            return psum.tile(shape, F32, name="b%d" % n)

        def ev_bank(e):
            c, b = divmod(e, 4)
            if b == 0:
                grp[c] = grps.tile([P, 4096], BF16, name="grp", align_bytes=64)
            xt = bank(e % 4, [P, 4, P])
            for a in range(2):
                for u in range(2):
                    nc.tensor.transpose(xt[:, 2 * a + u, :], x32[c][:, 2 * b + a, u * P:(u + 1) * P], ident[:])
            grf = grp[c][:].bitcast(F32).rearrange("p (b a r u) -> p b a r u", b=4, a=2, u=2)
            nc.scalar.copy(out=grf[:, b], in_=xt[:].rearrange("p (a u) r -> p a r u", u=2))

        def qx(c):
            cols = slice(c * CH * P, (c + 1) * CH * P)
            nc.vector.quantize_mx(out=xc[:, cols].bitcast(FP8X4), scales=xs[:, cols], in_=grp[c][:])

        def qgh(h):
            js = slice(GR * h, GR * h + GR)
            nc.vector.tensor_tensor(
                out=qtab[:, js, :].rearrange("p j (c i e) -> p (j c) i e", c=2, e=2),
                in0=base[:, js, :].rearrange("p j (c i) -> p (j c) i", c=2).unsqueeze(3).to_broadcast(
                    [P, 2 * GR, NPAIR, 2]),
                in1=gq[:].rearrange("p (i e) -> p i e", e=2).unsqueeze(1).to_broadcast([P, 2 * GR, NPAIR, 2]),
                op=ALU.mult)

        with tc.tile_pool(name="pro", bufs=1) as pro, tc.tile_pool(name="tabs", bufs=4) as tabs:
            w_sb = pro.tile([P, 3, D], BF16, name="w_sb")
            nc.scalar.dma_start(out=w_sb[:, 0:2, :], in_=wq.rearrange("(r p) k -> p r k", p=P))
            nc.scalar.dma_start(out=w_sb[:, 2, :], in_=wkv)
            nc.scalar.dma_start(out=gq_bf[:], in_=q_norm_w.partition_broadcast(P))
            nc.scalar.dma_start(out=gk_bf[:], in_=k_norm_w.partition_broadcast(P))
            for c in range(NCH):
                x_sb = xin.tile([P, CH, D], BF16, name="x_sb")
                nc.sync.dma_start(out=x_sb[:], in_=xv[:, c * CH:(c + 1) * CH, :])
                x32[c] = x_sb[:].bitcast(F32)

            make_identity(nc, ident[:])
            t1i = pro.tile([P, NCH], I32, name="t1i")
            nc.gpsimd.iota(t1i[:], pattern=[[CH, NCH]], base=0, channel_multiplier=NT)
            j0i = pro.tile([P, CH], I32, name="j0i")
            nc.gpsimd.iota(j0i[:], pattern=[[1, CH]], base=0, channel_multiplier=0)
            nc.vector.memset(ones[:], 1.0)
            nc.vector.memset(eps_t[:], EPS)
            his, los = turn_constants()
            fhi = pro.tile([P, NPAIR], F32, name="fhi")
            flo = pro.tile([P, NPAIR], F32, name="flo")
            for i in range(NPAIR):
                nc.vector.memset(fhi[:, i:i + 1], his[i])
                nc.scalar.activation(out=flo[:, i:i + 1], in_=ones[:], func=ACT.Copy, scale=los[i])
            idv = ident[:].rearrange("p (i e) -> p e i", e=2)
            pmv = perm[:].rearrange("p (i e) -> p e i", e=2)
            nc.vector.tensor_copy(out=pmv[:, 0], in_=idv[:, 1])
            nc.vector.tensor_copy(out=pmv[:, 1], in_=idv[:, 0])
            t1f = pro.tile([P, NCH], F32, name="t1f")
            j0f = pro.tile([P, CH], F32, name="j0f")
            nc.vector.tensor_copy(out=t1f[:], in_=t1i[:])
            nc.vector.tensor_copy(out=j0f[:], in_=j0i[:])

            w32 = w_sb[:].bitcast(F32)
            gw = pro.tile([P, WCOLS * 4], BF16, name="gw", align_bytes=64)
            gwf = gw[:].bitcast(F32).rearrange("p (c u) -> p c u", u=2)
            gwb = gw[:].rearrange("p (i e u f) -> p e i u f", e=2, u=2, f=2)

            def w_transposes(dst, slot, r, mat):
                for u in range(2):
                    nc.tensor.transpose(dst[:, slot + u, :], w32[:, r, u * P:(u + 1) * P], mat[:])

            def plain_cols(src, slot, cb):
                nc.scalar.copy(out=gwf[:, cb:cb + P, :], in_=src[:, slot:slot + 2, :].rearrange("p u c -> p c u"))

            def swapped_cols(src, slot, cb, n):
                sv = src[:, slot:slot + 2, 0:n].rearrange("p u (i e) -> p e i u", e=2)
                dv = gwf[:, cb:cb + n, :].rearrange("p (i e) u -> p e i u", e=2)
                nc.vector.tensor_copy(out=dv[:, 1], in_=sv[:, 1])
                sb = src[:].bitcast(BF16)[:, slot:slot + 2, 0:2 * n].rearrange("p u (i e f) -> p e i u f", e=2, f=2)
                nc.vector.tensor_scalar(out=gwb[:, 0, cb // 2:(cb + n) // 2], in0=sb[:, 0], scalar1=-1.0,
                                        scalar2=None, op0=ALU.mult)

            pa = bank(4, [P, 4, P])
            w_transposes(pa, 0, 0, ident)
            w_transposes(pa, 2, 1, ident)
            pb = bank(5, [P, 4, P])
            w_transposes(pb, 0, 2, ident)
            w_transposes(pb, 2, 2, perm)
            pc = bank(6, [P, 4, P])
            w_transposes(pc, 0, 0, perm)
            w_transposes(pc, 2, 1, perm)
            plain_cols(pa, 0, 256)
            plain_cols(pa, 2, 384)
            plain_cols(pb, 0, 576)

            def outer(dst, col, row):
                nc.vector.tensor_tensor(out=dst[:], in0=col[:].unsqueeze(2).to_broadcast([P, 8, NPAIR]),
                                        in1=row[:].unsqueeze(1).to_broadcast([P, 8, NPAIR]), op=ALU.mult)

            def flat(t):
                return t[:].rearrange("p a i -> p (a i)")

            uh = pro.tile([P, 8, NPAIR], F32, name="uh")
            ki = pro.tile([P, 8, NPAIR], I32, name="ki")
            kf = pro.tile([P, 8, NPAIR], F32, name="kf")
            ul = pro.tile([P, 8, NPAIR], F32, name="ul")
            na = pro.tile([P, 8, NPAIR], F32, name="na")
            bh = pro.tile([P, 8, NPAIR], F32, name="bh")
            bl = pro.tile([P, 8, NPAIR], F32, name="bl")
            bb = pro.tile([P, 8, 2, NPAIR], F32, name="bb")
            nb = pro.tile([P, 16, NPAIR], F32, name="nb")
            bbf = bb[:].rearrange("p a c i -> p (a c i)")
            outer(uh, t1f, fhi)
            outer(bh, j0f, fhi)
            nc.vector.tensor_copy(out=ki[:], in_=uh[:])
            outer(bl, j0f, flo)
            nc.vector.tensor_copy(out=kf[:], in_=ki[:])
            outer(ul, t1f, flo)
            nc.vector.tensor_tensor(out=uh[:], in0=uh[:], in1=kf[:], op=ALU.subtract)
            nc.vector.tensor_tensor(out=bb[:, :, 0, :], in0=bh[:], in1=bl[:], op=ALU.add)
            nc.vector.tensor_tensor(out=uh[:], in0=uh[:], in1=ul[:], op=ALU.add)
            nc.vector.tensor_scalar(out=bb[:, :, 1, :], in0=bb[:, :, 0, :], scalar1=0.25, scalar2=None, op0=ALU.add)
            nc.vector.scalar_tensor_tensor(out=flat(na), in0=flat(uh), scalar=0.5, in1=flat(uh), op0=ALU.is_ge,
                                           op1=ALU.subtract)
            nc.vector.scalar_tensor_tensor(out=flat(nb), in0=bbf, scalar=1.0, in1=bbf, op0=ALU.is_ge,
                                           op1=ALU.subtract)

            swapped_cols(pb, 2, 512, DH)
            swapped_cols(pc, 0, 0, P)
            swapped_cols(pc, 2, 128, P)

            for e in range(9):
                ev_bank(e)

            for c in range(NCH):
                nv = tabs.tile([P, 16, NPAIR], F32, name="nv")
                nc.gpsimd.tensor_tensor(out=nv[:], in0=nb[:],
                                        in1=na[:, c, :].unsqueeze(1).to_broadcast([P, 16, NPAIR]), op=ALU.add)
                if c >= 2:
                    qgh(c - 2)
                nc.vector.scalar_tensor_tensor(out=flat(nv), in0=flat(nv), scalar=-0.5, in1=flat(nv), op0=ALU.is_lt,
                                               op1=ALU.add)
                if c == 0:
                    nc.vector.quantize_mx(out=wc[:, 0:512].bitcast(FP8X4), scales=ws[:, 0:512], in_=gw[:, 0:2048])
                    nc.vector.quantize_mx(out=wc[:, 512:640].bitcast(FP8X4), scales=ws[:, 512:640],
                                          in_=gw[:, 2048:2560])
                    nc.vector.quantize_mx(out=wc[:, 640:704].bitcast(FP8X4), scales=ws[:, 640:704],
                                          in_=gw[:, 2560:2816])
                    nc.vector.tensor_copy(out=gq[:], in_=gq_bf[:])
                    nc.vector.tensor_copy(out=gk[:], in_=gk_bf[:])
                nc.scalar.activation(out=base[:, c * CH:(c + 1) * CH, :].rearrange("p j m -> p (j m)"), in_=flat(nv),
                                     func=ACT.Sin, scale=-TWO_PI)
                ev_bank(9 + c)

        for e in range(17, 32):
            ev_bank(e)
        for c in range(NCH):
            qx(c)

        work = ctx.enter_context(tc.tile_pool(name="work", bufs=2))
        outs = ctx.enter_context(tc.tile_pool(name="outs", bufs=2))

        ps_t = {}
        ss_t = {}
        rs_t = {}
        ov_t = {}
        oq_t = {}
        ok_t = {}
        tq_t = {}
        tk_t = {}
        pq_t = {}
        pk_t = {}

        def lhs_of(j):
            return xc[:, j * P:(j + 1) * P].bitcast(FP8X4), xs[:, j * P:(j + 1) * P]

        def m1(j):
            ps = bank(4 + j % 3, [P, 384])
            ps_t[j] = ps
            lhs, lsc = lhs_of(j)
            nc.tensor.matmul_mx(out=ps[:, 0:256], lhsT=lhs, lhsT_scale=lsc, rhs=wc[:, 256:512].bitcast(FP8X4),
                                rhs_scale=ws[:, 256:512], start=True, stop=True)
            nc.tensor.matmul_mx(out=ps[:, 256:384], lhsT=lhs, lhsT_scale=lsc, rhs=wc[:, 576:704].bitcast(FP8X4),
                                rhs_scale=ws[:, 576:704], start=True, stop=True)

        def squares(j):
            q, i = divmod(j, GR)
            c, jj = divmod(j, CH)
            if i == 0:
                ss_t[q] = small.tile([P, 5 * GR], F32, name="ss")
            if jj == 0:
                ov_t[c] = outs.tile([P, CH, DH], F32, name="ov", bufs=3)
            ps = ps_t[j]
            junk = junks.tile([P, 5, DH], BF16, name="junk")
            for h in range(5):
                nc.scalar.activation(out=junk[:, h, :], in_=ps[:, h * DH:(h + 1) * DH], func=ACT.Square,
                                     accum_out=ss_t[q][:, i * 5 + h:i * 5 + h + 1])
            nc.scalar.copy(out=ov_t[c][:, jj, :], in_=ps[:, 320:384])
            if i == GR - 1:
                rs_t[q] = small.tile([P, 5 * GR], F32, name="rs")
                nc.scalar.activation(out=rs_t[q][:], in_=ss_t[q][:], func=ACT.Abs_reciprocal_sqrt, scale=1.0 / DH,
                                     bias=eps_t[:])

        def m2q(j):
            pq = bank(j % 4, [P, 512])
            pq_t[j] = pq
            lhs, lsc = lhs_of(j)
            nc.tensor.matmul_mx(out=pq[:], lhsT=lhs, lhsT_scale=lsc, rhs=wc[:, 0:512].bitcast(FP8X4),
                                rhs_scale=ws[:, 0:512], start=True, stop=True)

        def m2k(q):
            pk = bank(7, [P, GR, 2 * DH])
            pk_t[q] = pk
            for i in range(GR):
                lhs, lsc = lhs_of(q * GR + i)
                nc.tensor.matmul_mx(out=pk[:, i, :], lhsT=lhs, lhsT_scale=lsc, rhs=wc[:, 512:640].bitcast(FP8X4),
                                    rhs_scale=ws[:, 512:640], start=True, stop=True)

        def rope(j):
            q, i = divmod(j, GR)
            c, jj = divmod(j, CH)
            if i == 0:
                tq_t[q] = work.tile([P, GR, 512], F32, name="tq", bufs=3)
            if jj == 0:
                tk_t[c] = work.tile([P, CH, 2 * DH], F32, name="tk")
            rs = rs_t[q]
            pv = pq_t[j][:].rearrange("p (c h d) -> p h c d", c=2, h=4)
            tv = tq_t[q][:, i, :].rearrange("p (c h d) -> p h c d", c=2, h=4)
            for h in range(4):
                nc.vector.scalar_tensor_tensor(out=tv[:, h], in0=pv[:, h], scalar=rs[:, i * 5 + h:i * 5 + h + 1],
                                               in1=qtab[:, j, :].rearrange("p (c d) -> p c d", c=2), op0=ALU.mult,
                                               op1=ALU.mult)
            nc.vector.scalar_tensor_tensor(
                out=tk_t[c][:, jj, :].rearrange("p (m e) -> p m e", e=2),
                in0=pk_t[q][:, i, :].rearrange("p (m e) -> p m e", e=2), scalar=rs[:, i * 5 + 4:i * 5 + 5],
                in1=base[:, j, :].unsqueeze(2).to_broadcast([P, 2 * NPAIR, 2]), op0=ALU.mult, op1=ALU.mult)

        def add_q(eng, q, lo, hi):
            c, half = divmod(q, 2)
            if half == 0 and lo == 0:
                oq_t[c] = outs.tile([P, 4, CH, DH], F32, name="oq")
            tq = tq_t[q]
            eng.tensor_tensor(
                out=oq_t[c][:, :, half * GR + lo:half * GR + hi, :].rearrange("p h j d -> p j h d"),
                in0=tq[:, lo:hi, 0:256].rearrange("p j (h d) -> p j h d", h=4),
                in1=tq[:, lo:hi, 256:512].rearrange("p j (h d) -> p j h d", h=4), op=ALU.add)

        def add_k(c, lo, hi):
            if lo == 0:
                ok_t[c] = outs.tile([P, CH, DH], F32, name="ok")
            uk = work.tile([P, CH, DH], F32, name="uk")
            nc.gpsimd.tensor_tensor(out=uk[:, lo:hi, :], in0=tk_t[c][:, lo:hi, 0:DH], in1=tk_t[c][:, lo:hi, DH:2 * DH],
                                    op=ALU.add)
            nc.gpsimd.tensor_tensor(out=ok_t[c][:, lo:hi, :], in0=uk[:, lo:hi, :],
                                    in1=gk[:].unsqueeze(1).to_broadcast([P, hi - lo, DH]), op=ALU.mult)

        def store(c, lo, hi):
            js = slice(c * CH + lo, c * CH + hi)
            nc.sync.dma_start(out=oqv[:, :, js, :], in_=oq_t[c][:, :, lo:hi, :])
            nc.sync.dma_start(out=okv[:, js, :], in_=ok_t[c][:, lo:hi, :])

        for a in range(D1):
            m1(a)
        for a in range(SL):
            m1(a + D1)
            squares(a)
        for j in range(D2):
            m2q(j)
        m2k(0)

        for q in range(NGR):
            if 6 + q < NGR:
                qgh(6 + q)
            for i in range(GR):
                j = q * GR + i
                a = j + SL
                if a + D1 < NT:
                    m1(a + D1)
                if i == 0 and q > 0:
                    m2k(q)
                if j + D2 < NT:
                    m2q(j + D2)
                if a < NT:
                    squares(a)
                    if a % CH == CH - 1:
                        nc.sync.dma_start(out=ovv[:, a - CH + 1:a + 1, :], in_=ov_t[a // CH][:])
                rope(j)
            c = q // 2
            add_q(nc.vector if (q % 4 == 3 or q >= NGR - 2) else nc.gpsimd, q, 0, GR)
            if q < NGR - 2:
                if q % 2 == 1:
                    add_k(c, 0, CH)
                    store(c, 0, CH)
            elif q == NGR - 2:
                add_k(c, 0, GR)
                store(c, 0, GR)
            else:
                add_k(c, GR, CH)
                store(c, GR, CH)
